import numpy as np
import ml_dtypes


def mxq(x, axis, fmt="e4m3"):
    dtype, down = {"e4m3": (ml_dtypes.float8_e4m3fn, 7), "e5m2": (ml_dtypes.float8_e5m2, 14)}[fmt]
    v = np.moveaxis(np.asarray(x, np.float32).astype(ml_dtypes.bfloat16).astype(np.float64), axis, -1)
    blocks = v.reshape(v.shape[:-1] + (-1, 32))
    amax = np.abs(blocks).max(-1, keepdims=True)
    byte = np.maximum(np.where(amax > 0, np.frexp(amax)[1] - 1 + 127, 0) - down, 1)
    scale = np.exp2(byte - 127.0)
    codes = (blocks / scale).astype(np.float32).astype(dtype).astype(np.float64)
    return np.moveaxis((codes * scale).reshape(v.shape), -1, axis)


WIDE = False


def mx_kscale(k):
    if not WIDE:
        return np.ones(k)
    levels = np.array([10, -10, 5, -5, 0])
    if k % 512:
        return np.exp2(np.random.permutation(np.resize(levels, k // 32))).repeat(32)
    a = np.empty((k // 512, 16))
    for p in range(k // 512):
        a[p, :8] = np.random.permutation(np.resize(levels, 8))
        for g in range(8):
            far = levels[np.abs(levels - a[p, g]) >= 10]
            a[p, g + 8] = far[np.random.randint(len(far))]
    return np.exp2(a.ravel()).repeat(32)


BF16 = ml_dtypes.bfloat16


def bf(x):
    return np.asarray(x, np.float32).astype(BF16)


def f64(x):
    return np.asarray(x).astype(np.float64)


E, F, H, MID, OUT = 16384, 64, 192, 512, 128
D = 2 * (F + H)
IN = D + 1


def setup_inputs():
    s = mx_kscale(D)
    t = mx_kscale(MID)
    w1 = np.concatenate([np.random.standard_normal((MID, D)) / np.sqrt(D) / s[None, :],
                         np.random.standard_normal((MID, 1)) * 0.5], axis=1) * t[:, None]
    return {"dst_node_feat": bf(np.random.standard_normal((E, F)) * s[:F]),
            "dst_node_hidden": bf(np.random.standard_normal((E, H)) * s[F:F + H]),
            "src_node_feat": bf(np.random.standard_normal((E, F)) * s[F + H:2 * F + H]),
            "src_node_hidden": bf(np.random.standard_normal((E, H)) * s[2 * F + H:]),
            "edge_feat": bf(np.random.standard_normal(E)),
            "W1": bf(w1),
            "b1": bf(np.random.standard_normal(MID) * 0.3 * t),
            "W2": bf(np.random.standard_normal((OUT, MID)) / np.sqrt(MID) / t[None, :]),
            "b2": bf(np.random.standard_normal(OUT) * 0.3)}


def reference(dst_node_feat, dst_node_hidden, src_node_feat, src_node_hidden, edge_feat, W1, b1, W2, b2):
    x = np.concatenate([f64(dst_node_feat), f64(dst_node_hidden), f64(src_node_feat), f64(src_node_hidden),
                        f64(edge_feat)[:, None]], axis=1)
    w1 = f64(W1)
    pre = (mxq(x[:, :D], 1, "e4m3") @ mxq(w1[:, :D], 1, "e4m3").T) + x[:, D:] * w1[:, D] + f64(b1)
    h = np.maximum(pre, 0.0)
    return np.tanh((mxq(h, 1, "e4m3") @ mxq(f64(W2), 1, "e4m3").T) + f64(b2))

@@ -1,0 +1,287 @@
+from contextlib import ExitStack
+
+import concourse.mybir as mybir
+from concourse.masks import make_identity
+
+F32 = mybir.dt.float32
+BF16 = mybir.dt.bfloat16
+U32 = mybir.dt.uint32
+U8 = mybir.dt.uint8
+FP8X4 = mybir.dt.float8_e4m3fn_x4
+ACT = mybir.ActivationFunctionType
+ALU = mybir.AluOpType
+
+P = 128
+PACK = 4
+E, F, H, MID, OUT = 16384, 64, 192, 512, 128
+D = 2 * (F + H)
+M_TILES = MID // P
+CHUNK = 512
+SUBS = CHUNK // P
+N_CHUNKS = E // CHUNK
+CHUNKS_AHEAD = 4
+EDGE_PIECE = 2048
+CHUNKS_PER_PIECE = EDGE_PIECE // CHUNK
+RUN = 4
+SCALAR_M_TILES = 1
+SCALAR_EDGES = P
+
+FLOPS = 2 * E * ((D + 1) * MID + MID * OUT)
+
+
+def tile_edgenetwork_kernel(
+    tc,
+    dst_node_feat,
+    dst_node_hidden,
+    src_node_feat,
+    src_node_hidden,
+    edge_feat,
+    W1,
+    b1,
+    W2,
+    b2,
+    out,
+):
+    nc = tc.nc
+    with ExitStack() as stack:
+        stack.enter_context(tc.manual_schedule())
+        const = stack.enter_context(tc.tile_pool(name="const", bufs=1))
+        rows_pool = stack.enter_context(tc.tile_pool(name="rows", bufs=CHUNKS_AHEAD + 1))
+        term_pool = stack.enter_context(tc.tile_pool(name="term", bufs=3))
+        work = stack.enter_context(tc.tile_pool(name="work", bufs=2))
+        store_pool = stack.enter_context(tc.tile_pool(name="store", bufs=3))
+        flip_psum = stack.enter_context(tc.psum_pool(name="flip_psum", bufs=2))
+        layer1_psum = stack.enter_context(tc.psum_pool(name="layer1_psum", bufs=M_TILES))
+        layer2_psum = stack.enter_context(tc.psum_pool(name="layer2_psum", bufs=1))
+        back_psum = stack.enter_context(tc.psum_pool(name="back_psum", bufs=1))
+
+        x_parts = (
+            (dst_node_feat, 0, F),
+            (dst_node_hidden, F, H),
+            (src_node_feat, F + H, F),
+            (src_node_hidden, 2 * F + H, H),
+        )
+        x_rows = {}
+
+        def load_chunk(c):
+            rows = rows_pool.tile([P, SUBS, D], BF16, name="x_rows")
+            for part, first, width in x_parts:
+                nc.sync.dma_start(
+                    out=rows[:, :, first : first + width],
+                    in_=part[c * CHUNK : (c + 1) * CHUNK, :].rearrange("(s p) k -> p s k", p=P),
+                )
+            x_rows[c] = rows
+
+        edge_all = const.tile([P, E], BF16)
+
+        def load_edges(q):
+            nc.sync.dma_start(
+                out=edge_all[:, q * EDGE_PIECE : (q + 1) * EDGE_PIECE],
+                in_=edge_feat[q * EDGE_PIECE : (q + 1) * EDGE_PIECE].partition_broadcast(P),
+            )
+
+        w1_rows = const.tile([P, M_TILES, D + 2], BF16)
+        nc.sync.dma_start(out=w1_rows[:, :, 0 : D + 1], in_=W1.rearrange("(p t) k -> p t k", t=M_TILES))
+        load_chunk(0)
+        load_edges(0)
+        w2_rows = const.tile([P, MID], BF16)
+        nc.sync.dma_start(out=w2_rows[:], in_=W2)
+        b1_in = const.tile([P, M_TILES], BF16)
+        nc.sync.dma_start(out=b1_in[:], in_=b1.rearrange("(p t) -> p t", t=M_TILES))
+        bias_rows = const.tile([P, P], BF16)
+        nc.vector.memset(bias_rows[:], 0.0)
+        nc.sync.dma_start(out=bias_rows[0:1, :], in_=b2.rearrange("(o p) -> o p", p=P))
+        for c in range(1, CHUNKS_AHEAD):
+            load_chunk(c)
+
+        ident_f32 = const.tile([P, P], F32)
+        make_identity(nc, ident_f32[:])
+        ident_bf16 = const.tile([P, P], BF16)
+        make_identity(nc, ident_bf16[:])
+
+        def contraction_onto_partitions(row_words, grouped, half):
+            grouped_words = grouped[:].bitcast(F32)
+            flipped = flip_psum.tile([P, 2, 2, P], F32)
+            for s in range(2):
+                for u in range(2):
+                    nc.tensor.transpose(
+                        flipped[:, s, u, :], row_words(2 * half + s)[:, u : D // 2 : 2], ident_f32[:]
+                    )
+            nc.scalar.copy(
+                out=grouped_words[:, 2 * half * P : (2 * half + 2) * P, :].rearrange("p (s r) u -> p s r u", s=2),
+                in_=flipped[:].rearrange("p s u r -> p s r u"),
+            )
+
+        def quantise(grouped, codes, scales):
+            nc.vector.quantize_mx(
+                out=codes[:].bitcast(FP8X4), scales=scales[:], in_=grouped[:].rearrange("p c j -> p (c j)")
+            )
+
+        w1_words = w1_rows[:].bitcast(F32)
+        w1_grouped = const.tile([P, MID, PACK], BF16, align_bytes=64)
+        for half in range(2):
+            contraction_onto_partitions(lambda t: w1_words[:, t, 0 : D // 2], w1_grouped, half)
+        w1_codes = const.tile([P, MID], U32, align_bytes=64)
+        w1_scales = const.tile([P, MID], U8, align_bytes=64)
+        quantise(w1_grouped, w1_codes, w1_scales)
+
+        w2_words = w2_rows[:].bitcast(F32)
+        w2_flipped = back_psum.tile([P, 2, OUT], F32, tag="back")
+        for u in range(2):
+            nc.tensor.transpose(w2_flipped[:, u, :], w2_words[:, u : MID // 2 : 2], ident_f32[:])
+        w2_grouped = const.tile([P, OUT, PACK], BF16, align_bytes=64)
+        nc.vector.tensor_copy(out=w2_grouped[:].bitcast(F32), in_=w2_flipped[:].rearrange("p u o -> p o u"))
+        w2_codes = const.tile([P, OUT], U32, align_bytes=64)
+        w2_scales = const.tile([P, OUT], U8, align_bytes=64)
+
+        bias_flipped = layer2_psum.tile([P, P], BF16, tag="layer2")
+        nc.tensor.transpose(bias_flipped[:], bias_rows[:], ident_bf16[:])
+        bias_cols = const.tile([P, M_TILES + 1], F32)
+        nc.vector.tensor_copy(out=bias_cols[:, 0:M_TILES], in_=b1_in[:])
+        nc.vector.tensor_copy(out=bias_cols[:, M_TILES : M_TILES + 1], in_=bias_flipped[:, 0:1])
+        w1_last = const.tile([P, M_TILES], F32)
+        nc.vector.tensor_copy(out=w1_last[:], in_=w1_rows[:, :, D])
+        quantise(w2_grouped, w2_codes, w2_scales)
+
+        x_grouped, x_codes, x_scales = {}, {}, {}
+        edge_terms, layer1_banks, pre_acts, hidden = {}, {}, {}, {}
+        h_codes, h_scales, out_flipped, out_back = {}, {}, {}, {}
+
+        def flip_x(c, half):
+            x_words = x_rows[c][:].bitcast(F32)
+            if half == 0:
+                x_grouped[c] = work.tile([P, CHUNK, PACK], BF16, align_bytes=64, name="x_grouped")
+            contraction_onto_partitions(lambda s: x_words[:, s, :], x_grouped[c], half)
+
+        def make_edge_term(c):
+            term = term_pool.tile([P, M_TILES, CHUNK], F32, name="edge_term")
+            edges = edge_all[:, c * CHUNK : (c + 1) * CHUNK]
+            for t in range(M_TILES):
+                if t < SCALAR_M_TILES:
+                    nc.scalar.activation(
+                        out=term[:, t, :],
+                        in_=edges,
+                        func=ACT.Identity,
+                        scale=w1_last[:, t : t + 1],
+                        bias=bias_cols[:, t : t + 1],
+                    )
+                else:
+                    nc.gpsimd.tensor_scalar(
+                        out=term[:, t, :],
+                        in0=edges,
+                        scalar1=w1_last[:, t : t + 1],
+                        scalar2=bias_cols[:, t : t + 1],
+                        op0=ALU.mult,
+                        op1=ALU.add,
+                    )
+            edge_terms[c] = term
+
+        def quantise_x(c):
+            codes = work.tile([P, CHUNK], U32, align_bytes=64, name="x_codes")
+            scales = work.tile([P, CHUNK], U8, align_bytes=64, name="x_scales")
+            quantise(x_grouped[c], codes, scales)
+            x_codes[c], x_scales[c] = codes, scales
+
+        def layer1(c, t):
+            bank = layer1_psum.tile([P, CHUNK], F32, name="layer1_bank")
+            nc.tensor.matmul_mx(
+                out=bank[:],
+                lhsT=w1_codes[:, t * P : (t + 1) * P].bitcast(FP8X4),
+                lhsT_scale=w1_scales[:, t * P : (t + 1) * P],
+                rhs=x_codes[c][:].bitcast(FP8X4),
+                rhs_scale=x_scales[c][:],
+                start=True,
+                stop=True,
+            )
+            layer1_banks[c, t] = bank
+
+        def add_edge_term(c, t):
+            if t == 0:
+                pre_acts[c] = work.tile([P, M_TILES, CHUNK], BF16, name="pre_act")
+            nc.vector.tensor_tensor(
+                out=pre_acts[c][:, t, :], in0=layer1_banks[c, t][:], in1=edge_terms[c][:, t, :], op=ALU.add
+            )
+
+        def relu_and_group_on_scalar(c):
+            hidden[c] = work.tile([P, CHUNK, PACK], BF16, align_bytes=64, name="hidden")
+            nc.scalar.activation(
+                out=hidden[c][:, 0:SCALAR_EDGES, :].rearrange("p (g i) t -> p g t i", i=RUN),
+                in_=pre_acts[c][:, :, 0:SCALAR_EDGES].rearrange("p t (g i) -> p g t i", i=RUN),
+                func=ACT.Relu,
+            )
+
+        def relu_and_group_on_vector(c):
+            nc.vector.tensor_scalar_max(
+                out=hidden[c][:, SCALAR_EDGES:CHUNK, :].rearrange("p (g i) t -> p g t i", i=RUN),
+                in0=pre_acts[c][:, :, SCALAR_EDGES:CHUNK].rearrange("p t (g i) -> p g t i", i=RUN),
+                scalar1=0.0,
+            )
+
+        def quantise_h(c):
+            codes = work.tile([P, CHUNK], U32, align_bytes=64, name="h_codes")
+            scales = work.tile([P, CHUNK], U8, align_bytes=64, name="h_scales")
+            quantise(hidden[c], codes, scales)
+            h_codes[c], h_scales[c] = codes, scales
+
+        def layer2(c):
+            acc = layer2_psum.tile([P, CHUNK], F32, tag="layer2")
+            nc.tensor.matmul_mx(
+                out=acc[:],
+                lhsT=w2_codes[:].bitcast(FP8X4),
+                lhsT_scale=w2_scales[:],
+                rhs=h_codes[c][:].bitcast(FP8X4),
+                rhs_scale=h_scales[c][:],
+                start=True,
+                stop=True,
+            )
+            out_flipped[c] = work.tile([P, CHUNK], F32, name="out_flipped")
+            nc.scalar.activation(
+                out=out_flipped[c][:], in_=acc[:], func=ACT.Tanh, bias=bias_cols[:, M_TILES : M_TILES + 1], scale=1.0
+            )
+
+        def flip_back(c, half):
+            if half == 0:
+                out_back[c] = back_psum.tile([P, SUBS, OUT], F32, tag="back", name="out_back")
+            for s in (2 * half, 2 * half + 1):
+                nc.tensor.transpose(out_back[c][:, s, :], out_flipped[c][:, s * P : (s + 1) * P], ident_f32[:])
+
+        def store(c):
+            result = store_pool.tile([P, SUBS, OUT], F32)
+            nc.scalar.copy(out=result[:], in_=out_back[c][:])
+            nc.scalar.dma_start(
+                out=out[c * CHUNK : (c + 1) * CHUNK, :].rearrange("(s p) o -> p s o", p=P), in_=result[:]
+            )
+
+        def live(c):
+            return 0 <= c < N_CHUNKS
+
+        for i in range(-3, N_CHUNKS + 2):
+            ahead = i + 3
+            if live(ahead + CHUNKS_AHEAD):
+                load_chunk(ahead + CHUNKS_AHEAD)
+            if live(ahead + CHUNKS_PER_PIECE) and ahead % CHUNKS_PER_PIECE == 0:
+                load_edges(ahead // CHUNKS_PER_PIECE + 1)
+            for half in range(2):
+                if live(i):
+                    add_edge_term(i, 2 * half)
+                    add_edge_term(i, 2 * half + 1)
+                if half == 1 and live(i):
+                    relu_and_group_on_scalar(i)
+                if live(i + 1):
+                    layer1(i + 1, 2 * half)
+                    layer1(i + 1, 2 * half + 1)
+                if half == 1 and live(i - 1):
+                    quantise_h(i - 1)
+                    layer2(i - 1)
+                if live(i + 3):
+                    flip_x(i + 3, half)
+                if live(i - 2):
+                    flip_back(i - 2, half)
+            if live(i - 2):
+                store(i - 2)
+            if live(i + 2):
+                quantise_x(i + 2)
+            if live(i):
+                relu_and_group_on_vector(i)
+            if live(i + 2):
+                make_edge_term(i + 2)

@@ -23,7 +23,7 @@ CHUNKS_AHEAD = 4
 EDGE_PIECE = 2048
 CHUNKS_PER_PIECE = EDGE_PIECE // CHUNK
 RUN = 4
-SCALAR_M_TILES = 1
+GPSIMD_M_TILES = 3
 SCALAR_EDGES = P
 
 FLOPS = 2 * E * ((D + 1) * MID + MID * OUT)
@@ -47,7 +47,7 @@ def tile_edgenetwork_kernel(
         stack.enter_context(tc.manual_schedule())
         const = stack.enter_context(tc.tile_pool(name="const", bufs=1))
         rows_pool = stack.enter_context(tc.tile_pool(name="rows", bufs=CHUNKS_AHEAD + 1))
-        term_pool = stack.enter_context(tc.tile_pool(name="term", bufs=3))
+        term_pool = stack.enter_context(tc.tile_pool(name="term", bufs=2))
         work = stack.enter_context(tc.tile_pool(name="work", bufs=2))
         store_pool = stack.enter_context(tc.tile_pool(name="store", bufs=3))
         flip_psum = stack.enter_context(tc.psum_pool(name="flip_psum", bufs=2))
@@ -154,12 +154,13 @@ def tile_edgenetwork_kernel(
             contraction_onto_partitions(lambda s: x_words[:, s, :], x_grouped[c], half)
 
         def make_edge_term(c):
-            term = term_pool.tile([P, M_TILES, CHUNK], F32, name="edge_term")
             edges = edge_all[:, c * CHUNK : (c + 1) * CHUNK]
             for t in range(M_TILES):
-                if t < SCALAR_M_TILES:
+                term = term_pool.tile([P, CHUNK], F32, name=f"edge_term_{t}")
+                edge_terms[c, t] = term
+                if t >= GPSIMD_M_TILES:
                     nc.scalar.activation(
-                        out=term[:, t, :],
+                        out=term[:],
                         in_=edges,
                         func=ACT.Identity,
                         scale=w1_last[:, t : t + 1],
@@ -167,14 +168,13 @@ def tile_edgenetwork_kernel(
                     )
                 else:
                     nc.gpsimd.tensor_scalar(
-                        out=term[:, t, :],
+                        out=term[:],
                         in0=edges,
                         scalar1=w1_last[:, t : t + 1],
                         scalar2=bias_cols[:, t : t + 1],
                         op0=ALU.mult,
                         op1=ALU.add,
                     )
-            edge_terms[c] = term
 
         def quantise_x(c):
             codes = work.tile([P, CHUNK], U32, align_bytes=64, name="x_codes")
@@ -199,7 +199,7 @@ def tile_edgenetwork_kernel(
             if t == 0:
                 pre_acts[c] = work.tile([P, M_TILES, CHUNK], BF16, name="pre_act")
             nc.vector.tensor_tensor(
-                out=pre_acts[c][:, t, :], in0=layer1_banks[c, t][:], in1=edge_terms[c][:, t, :], op=ALU.add
+                out=pre_acts[c][:, t, :], in0=layer1_banks[c, t][:], in1=edge_terms[c, t][:], op=ALU.add
             )
 
         def relu_and_group_on_scalar(c):

@@ -22,9 +22,9 @@ N_CHUNKS = E // CHUNK
 CHUNKS_AHEAD = 4
 EDGE_PIECE = 2048
 CHUNKS_PER_PIECE = EDGE_PIECE // CHUNK
-RUN = 4
+RUN = 2
+TERM_LEAD = 1
 GPSIMD_M_TILES = 3
-SCALAR_EDGES = P
 
 FLOPS = 2 * E * ((D + 1) * MID + MID * OUT)
 
@@ -154,13 +154,16 @@ def tile_edgenetwork_kernel(
             contraction_onto_partitions(lambda s: x_words[:, s, :], x_grouped[c], half)
 
         def make_edge_term(c):
-            edges = edge_all[:, c * CHUNK : (c + 1) * CHUNK]
+            term = term_pool.tile([P, M_TILES, CHUNK], F32, name="edge_term")
+            edge_terms[c] = term
+            first = c * CHUNK - (SUBS - TERM_LEAD) * P
+            skip = max(0, -first)
+            width = min(E - first, CHUNK)
+            edges = edge_all[:, first + skip : first + width]
             for t in range(M_TILES):
-                term = term_pool.tile([P, CHUNK], F32, name=f"edge_term_{t}")
-                edge_terms[c, t] = term
                 if t >= GPSIMD_M_TILES:
                     nc.scalar.activation(
-                        out=term[:],
+                        out=term[:, t, skip:width],
                         in_=edges,
                         func=ACT.Identity,
                         scale=w1_last[:, t : t + 1],
@@ -168,7 +171,7 @@ def tile_edgenetwork_kernel(
                     )
                 else:
                     nc.gpsimd.tensor_scalar(
-                        out=term[:],
+                        out=term[:, t, skip:width],
                         in0=edges,
                         scalar1=w1_last[:, t : t + 1],
                         scalar2=bias_cols[:, t : t + 1],
@@ -182,40 +185,35 @@ def tile_edgenetwork_kernel(
             quantise(x_grouped[c], codes, scales)
             x_codes[c], x_scales[c] = codes, scales
 
-        def layer1(c, t):
-            bank = layer1_psum.tile([P, CHUNK], F32, name="layer1_bank")
-            nc.tensor.matmul_mx(
-                out=bank[:],
-                lhsT=w1_codes[:, t * P : (t + 1) * P].bitcast(FP8X4),
-                lhsT_scale=w1_scales[:, t * P : (t + 1) * P],
-                rhs=x_codes[c][:].bitcast(FP8X4),
-                rhs_scale=x_scales[c][:],
-                start=True,
-                stop=True,
-            )
-            layer1_banks[c, t] = bank
+        def layer1(c, s):
+            bank = layer1_psum.tile([P, M_TILES, P], F32, name="layer1_bank")
+            for t in range(M_TILES):
+                nc.tensor.matmul_mx(
+                    out=bank[:, t, :],
+                    lhsT=w1_codes[:, t * P : (t + 1) * P].bitcast(FP8X4),
+                    lhsT_scale=w1_scales[:, t * P : (t + 1) * P],
+                    rhs=x_codes[c][:, s * P : (s + 1) * P].bitcast(FP8X4),
+                    rhs_scale=x_scales[c][:, s * P : (s + 1) * P],
+                    start=True,
+                    stop=True,
+                )
+            layer1_banks[c, s] = bank
 
-        def add_edge_term(c, t):
-            if t == 0:
-                pre_acts[c] = work.tile([P, M_TILES, CHUNK], BF16, name="pre_act")
+        def add_edge_term(c, s):
+            if s == 0:
+                pre_acts[c] = work.tile([P, CHUNK, PACK], BF16, align_bytes=64, name="pre_act")
+            piece, first = divmod(c * SUBS + s + SUBS - TERM_LEAD, SUBS)
+            term = edge_terms[piece][:, :, first * P : (first + 1) * P]
             nc.vector.tensor_tensor(
-                out=pre_acts[c][:, t, :], in0=layer1_banks[c, t][:], in1=edge_terms[c, t][:], op=ALU.add
+                out=pre_acts[c][:, s * P : (s + 1) * P, :].rearrange("p (g i) t -> p g t i", i=RUN),
+                in0=layer1_banks[c, s][:].rearrange("p t (g i) -> p g t i", i=RUN),
+                in1=term.rearrange("p t (g i) -> p g t i", i=RUN),
+                op=ALU.add,
             )
 
-        def relu_and_group_on_scalar(c):
+        def relu(c):
             hidden[c] = work.tile([P, CHUNK, PACK], BF16, align_bytes=64, name="hidden")
-            nc.scalar.activation(
-                out=hidden[c][:, 0:SCALAR_EDGES, :].rearrange("p (g i) t -> p g t i", i=RUN),
-                in_=pre_acts[c][:, :, 0:SCALAR_EDGES].rearrange("p t (g i) -> p g t i", i=RUN),
-                func=ACT.Relu,
-            )
-
-        def relu_and_group_on_vector(c):
-            nc.vector.tensor_scalar_max(
-                out=hidden[c][:, SCALAR_EDGES:CHUNK, :].rearrange("p (g i) t -> p g t i", i=RUN),
-                in0=pre_acts[c][:, :, SCALAR_EDGES:CHUNK].rearrange("p t (g i) -> p g t i", i=RUN),
-                scalar1=0.0,
-            )
+            nc.vector.tensor_scalar_max(out=hidden[c][:], in0=pre_acts[c][:], scalar1=0.0)
 
         def quantise_h(c):
             codes = work.tile([P, CHUNK], U32, align_bytes=64, name="h_codes")
@@ -265,8 +263,6 @@ def tile_edgenetwork_kernel(
                 if live(i):
                     add_edge_term(i, 2 * half)
                     add_edge_term(i, 2 * half + 1)
-                if half == 1 and live(i):
-                    relu_and_group_on_scalar(i)
                 if live(i + 1):
                     layer1(i + 1, 2 * half)
                     layer1(i + 1, 2 * half + 1)
@@ -282,6 +278,6 @@ def tile_edgenetwork_kernel(
             if live(i + 2):
                 quantise_x(i + 2)
             if live(i):
-                relu_and_group_on_vector(i)
-            if live(i + 2):
+                relu(i)
+            if 0 <= i + 2 <= N_CHUNKS:
                 make_edge_term(i + 2)

@@ -47,7 +47,7 @@ def tile_edgenetwork_kernel(
         stack.enter_context(tc.manual_schedule())
         const = stack.enter_context(tc.tile_pool(name="const", bufs=1))
         rows_pool = stack.enter_context(tc.tile_pool(name="rows", bufs=CHUNKS_AHEAD + 1))
-        term_pool = stack.enter_context(tc.tile_pool(name="term", bufs=2))
+        term_pool = stack.enter_context(tc.tile_pool(name="term", bufs=3))
         work = stack.enter_context(tc.tile_pool(name="work", bufs=2))
         store_pool = stack.enter_context(tc.tile_pool(name="store", bufs=3))
         flip_psum = stack.enter_context(tc.psum_pool(name="flip_psum", bufs=2))
@@ -279,5 +279,5 @@ def tile_edgenetwork_kernel(
                 quantise_x(i + 2)
             if live(i):
                 relu(i)
-            if 0 <= i + 2 <= N_CHUNKS:
-                make_edge_term(i + 2)
+            if 0 <= i + 3 <= N_CHUNKS:
+                make_edge_term(i + 3)

@@ -22,7 +22,7 @@ N_CHUNKS = E // CHUNK
 CHUNKS_AHEAD = 4
 EDGE_PIECE = 2048
 CHUNKS_PER_PIECE = EDGE_PIECE // CHUNK
-RUN = 2
+RUN = 4
 TERM_LEAD = 1
 GPSIMD_M_TILES = 3
 
@@ -82,24 +82,21 @@ def tile_edgenetwork_kernel(
 
         w1_rows = const.tile([P, M_TILES, D + 2], BF16)
         nc.sync.dma_start(out=w1_rows[:, :, 0 : D + 1], in_=W1.rearrange("(p t) k -> p t k", t=M_TILES))
+        b1_in = const.tile([P, M_TILES], BF16)
+        nc.sync.dma_start(out=b1_in[:], in_=b1.rearrange("(p t) -> p t", t=M_TILES))
         load_chunk(0)
         load_edges(0)
         w2_rows = const.tile([P, MID], BF16)
         nc.sync.dma_start(out=w2_rows[:], in_=W2)
-        b1_in = const.tile([P, M_TILES], BF16)
-        nc.sync.dma_start(out=b1_in[:], in_=b1.rearrange("(p t) -> p t", t=M_TILES))
-        bias_rows = const.tile([P, P], BF16)
-        nc.vector.memset(bias_rows[:], 0.0)
-        nc.sync.dma_start(out=bias_rows[0:1, :], in_=b2.rearrange("(o p) -> o p", p=P))
+        b2_in = const.tile([P, 1], BF16)
+        nc.sync.dma_start(out=b2_in[:], in_=b2.rearrange("(p o) -> p o", o=1))
         for c in range(1, CHUNKS_AHEAD):
             load_chunk(c)
 
         ident_f32 = const.tile([P, P], F32)
         make_identity(nc, ident_f32[:])
-        ident_bf16 = const.tile([P, P], BF16)
-        make_identity(nc, ident_bf16[:])
 
-        def contraction_onto_partitions(row_words, grouped, half):
+        def contraction_onto_partitions(row_words, grouped, half, copy):
             grouped_words = grouped[:].bitcast(F32)
             flipped = flip_psum.tile([P, 2, 2, P], F32)
             for s in range(2):
@@ -107,7 +104,7 @@ def tile_edgenetwork_kernel(
                     nc.tensor.transpose(
                         flipped[:, s, u, :], row_words(2 * half + s)[:, u : D // 2 : 2], ident_f32[:]
                     )
-            nc.scalar.copy(
+            copy(
                 out=grouped_words[:, 2 * half * P : (2 * half + 2) * P, :].rearrange("p (s r) u -> p s r u", s=2),
                 in_=flipped[:].rearrange("p s u r -> p s r u"),
             )
@@ -117,31 +114,31 @@ def tile_edgenetwork_kernel(
                 out=codes[:].bitcast(FP8X4), scales=scales[:], in_=grouped[:].rearrange("p c j -> p (c j)")
             )
 
+        w1_last = const.tile([P, M_TILES], F32)
+        nc.vector.tensor_copy(out=w1_last[:], in_=w1_rows[:, :, D])
+        b1_cols = const.tile([P, M_TILES], F32)
+        nc.vector.tensor_copy(out=b1_cols[:], in_=b1_in[:])
         w1_words = w1_rows[:].bitcast(F32)
         w1_grouped = const.tile([P, MID, PACK], BF16, align_bytes=64)
         for half in range(2):
-            contraction_onto_partitions(lambda t: w1_words[:, t, 0 : D // 2], w1_grouped, half)
+            contraction_onto_partitions(lambda t: w1_words[:, t, 0 : D // 2], w1_grouped, half, nc.vector.tensor_copy)
         w1_codes = const.tile([P, MID], U32, align_bytes=64)
         w1_scales = const.tile([P, MID], U8, align_bytes=64)
         quantise(w1_grouped, w1_codes, w1_scales)
 
-        w2_words = w2_rows[:].bitcast(F32)
-        w2_flipped = back_psum.tile([P, 2, OUT], F32, tag="back")
-        for u in range(2):
-            nc.tensor.transpose(w2_flipped[:, u, :], w2_words[:, u : MID // 2 : 2], ident_f32[:])
+        b2_col = const.tile([P, 1], F32)
         w2_grouped = const.tile([P, OUT, PACK], BF16, align_bytes=64)
-        nc.vector.tensor_copy(out=w2_grouped[:].bitcast(F32), in_=w2_flipped[:].rearrange("p u o -> p o u"))
         w2_codes = const.tile([P, OUT], U32, align_bytes=64)
         w2_scales = const.tile([P, OUT], U8, align_bytes=64)
 
-        bias_flipped = layer2_psum.tile([P, P], BF16, tag="layer2")
-        nc.tensor.transpose(bias_flipped[:], bias_rows[:], ident_bf16[:])
-        bias_cols = const.tile([P, M_TILES + 1], F32)
-        nc.vector.tensor_copy(out=bias_cols[:, 0:M_TILES], in_=b1_in[:])
-        nc.vector.tensor_copy(out=bias_cols[:, M_TILES : M_TILES + 1], in_=bias_flipped[:, 0:1])
-        w1_last = const.tile([P, M_TILES], F32)
-        nc.vector.tensor_copy(out=w1_last[:], in_=w1_rows[:, :, D])
-        quantise(w2_grouped, w2_codes, w2_scales)
+        def prepare_layer2():
+            w2_words = w2_rows[:].bitcast(F32)
+            w2_flipped = back_psum.tile([P, 2, OUT], F32, tag="back", name="w2_flipped")
+            for u in range(2):
+                nc.tensor.transpose(w2_flipped[:, u, :], w2_words[:, u : MID // 2 : 2], ident_f32[:])
+            nc.vector.tensor_copy(out=w2_grouped[:].bitcast(F32), in_=w2_flipped[:].rearrange("p u o -> p o u"))
+            nc.vector.tensor_copy(out=b2_col[:], in_=b2_in[:])
+            quantise(w2_grouped, w2_codes, w2_scales)
 
         x_grouped, x_codes, x_scales = {}, {}, {}
         edge_terms, layer1_banks, pre_acts, hidden = {}, {}, {}, {}
@@ -151,7 +148,7 @@ def tile_edgenetwork_kernel(
             x_words = x_rows[c][:].bitcast(F32)
             if half == 0:
                 x_grouped[c] = work.tile([P, CHUNK, PACK], BF16, align_bytes=64, name="x_grouped")
-            contraction_onto_partitions(lambda s: x_words[:, s, :], x_grouped[c], half)
+            contraction_onto_partitions(lambda s: x_words[:, s, :], x_grouped[c], half, nc.scalar.copy)
 
         def make_edge_term(c):
             term = term_pool.tile([P, M_TILES, CHUNK], F32, name="edge_term")
@@ -167,14 +164,14 @@ def tile_edgenetwork_kernel(
                         in_=edges,
                         func=ACT.Identity,
                         scale=w1_last[:, t : t + 1],
-                        bias=bias_cols[:, t : t + 1],
+                        bias=b1_cols[:, t : t + 1],
                     )
                 else:
                     nc.gpsimd.tensor_scalar(
                         out=term[:, t, skip:width],
                         in0=edges,
                         scalar1=w1_last[:, t : t + 1],
-                        scalar2=bias_cols[:, t : t + 1],
+                        scalar2=b1_cols[:, t : t + 1],
                         op0=ALU.mult,
                         op1=ALU.add,
                     )
@@ -234,7 +231,7 @@ def tile_edgenetwork_kernel(
             )
             out_flipped[c] = work.tile([P, CHUNK], F32, name="out_flipped")
             nc.scalar.activation(
-                out=out_flipped[c][:], in_=acc[:], func=ACT.Tanh, bias=bias_cols[:, M_TILES : M_TILES + 1], scale=1.0
+                out=out_flipped[c][:], in_=acc[:], func=ACT.Tanh, bias=b2_col[:], scale=1.0
             )
 
         def flip_back(c, half):
@@ -279,5 +276,7 @@ def tile_edgenetwork_kernel(
                 quantise_x(i + 2)
             if live(i):
                 relu(i)
+            if i == -2:
+                prepare_layer2()
             if 0 <= i + 3 <= N_CHUNKS:
                 make_edge_term(i + 3)

@@ -23,8 +23,7 @@ CHUNKS_AHEAD = 4
 EDGE_PIECE = 2048
 CHUNKS_PER_PIECE = EDGE_PIECE // CHUNK
 RUN = 4
-TERM_LEAD = 1
-GPSIMD_M_TILES = 3
+GPSIMD_M_TILES = 2
 
 FLOPS = 2 * E * ((D + 1) * MID + MID * OUT)
 
@@ -68,7 +67,7 @@ def tile_edgenetwork_kernel(
             for part, first, width in x_parts:
                 nc.sync.dma_start(
                     out=rows[:, :, first : first + width],
-                    in_=part[c * CHUNK : (c + 1) * CHUNK, :].rearrange("(s p) k -> p s k", p=P),
+                    in_=part[c * CHUNK : (c + 1) * CHUNK, :].rearrange("(p s) k -> p s k", p=P),
                 )
             x_rows[c] = rows
 
@@ -151,16 +150,13 @@ def tile_edgenetwork_kernel(
             contraction_onto_partitions(lambda s: x_words[:, s, :], x_grouped[c], half, nc.scalar.copy)
 
         def make_edge_term(c):
-            term = term_pool.tile([P, M_TILES, CHUNK], F32, name="edge_term")
+            term = term_pool.tile([P, M_TILES, SUBS, P], F32, name="edge_term")
             edge_terms[c] = term
-            first = c * CHUNK - (SUBS - TERM_LEAD) * P
-            skip = max(0, -first)
-            width = min(E - first, CHUNK)
-            edges = edge_all[:, first + skip : first + width]
+            edges = edge_all[:, c * CHUNK : (c + 1) * CHUNK].rearrange("p (r s) -> p s r", s=SUBS)
             for t in range(M_TILES):
                 if t >= GPSIMD_M_TILES:
                     nc.scalar.activation(
-                        out=term[:, t, skip:width],
+                        out=term[:, t, :, :],
                         in_=edges,
                         func=ACT.Identity,
                         scale=w1_last[:, t : t + 1],
@@ -168,7 +164,7 @@ def tile_edgenetwork_kernel(
                     )
                 else:
                     nc.gpsimd.tensor_scalar(
-                        out=term[:, t, skip:width],
+                        out=term[:, t, :, :],
                         in0=edges,
                         scalar1=w1_last[:, t : t + 1],
                         scalar2=b1_cols[:, t : t + 1],
@@ -199,12 +195,10 @@ def tile_edgenetwork_kernel(
         def add_edge_term(c, s):
             if s == 0:
                 pre_acts[c] = work.tile([P, CHUNK, PACK], BF16, align_bytes=64, name="pre_act")
-            piece, first = divmod(c * SUBS + s + SUBS - TERM_LEAD, SUBS)
-            term = edge_terms[piece][:, :, first * P : (first + 1) * P]
             nc.vector.tensor_tensor(
                 out=pre_acts[c][:, s * P : (s + 1) * P, :].rearrange("p (g i) t -> p g t i", i=RUN),
                 in0=layer1_banks[c, s][:].rearrange("p t (g i) -> p g t i", i=RUN),
-                in1=term.rearrange("p t (g i) -> p g t i", i=RUN),
+                in1=edge_terms[c][:, :, s, :].rearrange("p t (g i) -> p g t i", i=RUN),
                 op=ALU.add,
             )
 
@@ -244,7 +238,7 @@ def tile_edgenetwork_kernel(
             result = store_pool.tile([P, SUBS, OUT], F32)
             nc.scalar.copy(out=result[:], in_=out_back[c][:])
             nc.scalar.dma_start(
-                out=out[c * CHUNK : (c + 1) * CHUNK, :].rearrange("(s p) o -> p s o", p=P), in_=result[:]
+                out=out[c * CHUNK : (c + 1) * CHUNK, :].rearrange("(p s) o -> p s o", p=P), in_=result[:]
             )
 
         def live(c):
@@ -278,5 +272,5 @@ def tile_edgenetwork_kernel(
                 relu(i)
             if i == -2:
                 prepare_layer2()
-            if 0 <= i + 3 <= N_CHUNKS:
+            if live(i + 3):
                 make_edge_term(i + 3)

@@ -23,7 +23,9 @@ CHUNKS_AHEAD = 4
 EDGE_PIECE = 2048
 CHUNKS_PER_PIECE = EDGE_PIECE // CHUNK
 RUN = 4
-GPSIMD_M_TILES = 2
+GPSIMD_M_TILES = 3
+TERM_CHUNKS = 2
+SCALAR_RELU_SUBS = 1
 
 FLOPS = 2 * E * ((D + 1) * MID + MID * OUT)
 
@@ -46,7 +48,7 @@ def tile_edgenetwork_kernel(
         stack.enter_context(tc.manual_schedule())
         const = stack.enter_context(tc.tile_pool(name="const", bufs=1))
         rows_pool = stack.enter_context(tc.tile_pool(name="rows", bufs=CHUNKS_AHEAD + 1))
-        term_pool = stack.enter_context(tc.tile_pool(name="term", bufs=3))
+        term_pool = stack.enter_context(tc.tile_pool(name="term", bufs=2))
         work = stack.enter_context(tc.tile_pool(name="work", bufs=2))
         store_pool = stack.enter_context(tc.tile_pool(name="store", bufs=3))
         flip_psum = stack.enter_context(tc.psum_pool(name="flip_psum", bufs=2))
@@ -95,8 +97,9 @@ def tile_edgenetwork_kernel(
         ident_f32 = const.tile([P, P], F32)
         make_identity(nc, ident_f32[:])
 
-        def contraction_onto_partitions(row_words, grouped, half, copy):
+        def contraction_onto_partitions(row_words, grouped, first, half, copy):
             grouped_words = grouped[:].bitcast(F32)
+            begin = first + 2 * half * P
             flipped = flip_psum.tile([P, 2, 2, P], F32)
             for s in range(2):
                 for u in range(2):
@@ -104,13 +107,15 @@ def tile_edgenetwork_kernel(
                         flipped[:, s, u, :], row_words(2 * half + s)[:, u : D // 2 : 2], ident_f32[:]
                     )
             copy(
-                out=grouped_words[:, 2 * half * P : (2 * half + 2) * P, :].rearrange("p (s r) u -> p s r u", s=2),
+                out=grouped_words[:, begin : begin + 2 * P, :].rearrange("p (s r) u -> p s r u", s=2),
                 in_=flipped[:].rearrange("p s u r -> p s r u"),
             )
 
-        def quantise(grouped, codes, scales):
+        def quantise(grouped, codes, scales, columns):
             nc.vector.quantize_mx(
-                out=codes[:].bitcast(FP8X4), scales=scales[:], in_=grouped[:].rearrange("p c j -> p (c j)")
+                out=codes[:, columns].bitcast(FP8X4),
+                scales=scales[:, columns],
+                in_=grouped[:, columns, :].rearrange("p c j -> p (c j)"),
             )
 
         w1_last = const.tile([P, M_TILES], F32)
@@ -120,10 +125,10 @@ def tile_edgenetwork_kernel(
         w1_words = w1_rows[:].bitcast(F32)
         w1_grouped = const.tile([P, MID, PACK], BF16, align_bytes=64)
         for half in range(2):
-            contraction_onto_partitions(lambda t: w1_words[:, t, 0 : D // 2], w1_grouped, half, nc.vector.tensor_copy)
+            contraction_onto_partitions(lambda t: w1_words[:, t, 0 : D // 2], w1_grouped, 0, half, nc.vector.tensor_copy)
         w1_codes = const.tile([P, MID], U32, align_bytes=64)
         w1_scales = const.tile([P, MID], U8, align_bytes=64)
-        quantise(w1_grouped, w1_codes, w1_scales)
+        quantise(w1_grouped, w1_codes, w1_scales, slice(0, MID))
 
         b2_col = const.tile([P, 1], F32)
         w2_grouped = const.tile([P, OUT, PACK], BF16, align_bytes=64)
@@ -137,26 +142,29 @@ def tile_edgenetwork_kernel(
                 nc.tensor.transpose(w2_flipped[:, u, :], w2_words[:, u : MID // 2 : 2], ident_f32[:])
             nc.vector.tensor_copy(out=w2_grouped[:].bitcast(F32), in_=w2_flipped[:].rearrange("p u o -> p o u"))
             nc.vector.tensor_copy(out=b2_col[:], in_=b2_in[:])
-            quantise(w2_grouped, w2_codes, w2_scales)
+            quantise(w2_grouped, w2_codes, w2_scales, slice(0, OUT))
 
-        x_grouped, x_codes, x_scales = {}, {}, {}
-        edge_terms, layer1_banks, pre_acts, hidden = {}, {}, {}, {}
-        h_codes, h_scales, out_flipped, out_back = {}, {}, {}, {}
+        grouped, codes, scales = {}, {}, {}
+        edge_terms, layer1_banks, pre_acts, out_flipped, out_back = {}, {}, {}, {}, {}
+
+        def live(c):
+            return 0 <= c < N_CHUNKS
 
         def flip_x(c, half):
             x_words = x_rows[c][:].bitcast(F32)
-            if half == 0:
-                x_grouped[c] = work.tile([P, CHUNK, PACK], BF16, align_bytes=64, name="x_grouped")
-            contraction_onto_partitions(lambda s: x_words[:, s, :], x_grouped[c], half, nc.scalar.copy)
+            contraction_onto_partitions(lambda s: x_words[:, s, :], grouped[c - 2], CHUNK, half, nc.scalar.copy)
 
         def make_edge_term(c):
-            term = term_pool.tile([P, M_TILES, SUBS, P], F32, name="edge_term")
-            edge_terms[c] = term
-            edges = edge_all[:, c * CHUNK : (c + 1) * CHUNK].rearrange("p (r s) -> p s r", s=SUBS)
+            term = term_pool.tile([P, M_TILES, TERM_CHUNKS, SUBS, P], F32, name="edge_term")
+            edges = edge_all[:, c * CHUNK : (c + TERM_CHUNKS) * CHUNK].rearrange(
+                "p (h r s) -> p h s r", h=TERM_CHUNKS, s=SUBS
+            )
+            for h in range(TERM_CHUNKS):
+                edge_terms[c + h] = term[:, :, h, :, :]
             for t in range(M_TILES):
                 if t >= GPSIMD_M_TILES:
                     nc.scalar.activation(
-                        out=term[:, t, :, :],
+                        out=term[:, t, :, :, :],
                         in_=edges,
                         func=ACT.Identity,
                         scale=w1_last[:, t : t + 1],
@@ -164,7 +172,7 @@ def tile_edgenetwork_kernel(
                     )
                 else:
                     nc.gpsimd.tensor_scalar(
-                        out=term[:, t, :, :],
+                        out=term[:, t, :, :, :],
                         in0=edges,
                         scalar1=w1_last[:, t : t + 1],
                         scalar2=b1_cols[:, t : t + 1],
@@ -172,21 +180,22 @@ def tile_edgenetwork_kernel(
                         op1=ALU.add,
                     )
 
-        def quantise_x(c):
-            codes = work.tile([P, CHUNK], U32, align_bytes=64, name="x_codes")
-            scales = work.tile([P, CHUNK], U8, align_bytes=64, name="x_scales")
-            quantise(x_grouped[c], codes, scales)
-            x_codes[c], x_scales[c] = codes, scales
+        def quantise_step(i):
+            codes[i] = work.tile([P, 2 * CHUNK], U32, align_bytes=64, name="codes")
+            scales[i] = work.tile([P, 2 * CHUNK], U8, align_bytes=64, name="scales")
+            columns = slice(0 if live(i - 1) else CHUNK, 2 * CHUNK if live(i + 2) else CHUNK)
+            quantise(grouped[i], codes[i], scales[i], columns)
 
         def layer1(c, s):
             bank = layer1_psum.tile([P, M_TILES, P], F32, name="layer1_bank")
+            edges = slice(CHUNK + s * P, CHUNK + (s + 1) * P)
             for t in range(M_TILES):
                 nc.tensor.matmul_mx(
                     out=bank[:, t, :],
                     lhsT=w1_codes[:, t * P : (t + 1) * P].bitcast(FP8X4),
                     lhsT_scale=w1_scales[:, t * P : (t + 1) * P],
-                    rhs=x_codes[c][:, s * P : (s + 1) * P].bitcast(FP8X4),
-                    rhs_scale=x_scales[c][:, s * P : (s + 1) * P],
+                    rhs=codes[c - 2][:, edges].bitcast(FP8X4),
+                    rhs_scale=scales[c - 2][:, edges],
                     start=True,
                     stop=True,
                 )
@@ -202,15 +211,13 @@ def tile_edgenetwork_kernel(
                 op=ALU.add,
             )
 
-        def relu(c):
-            hidden[c] = work.tile([P, CHUNK, PACK], BF16, align_bytes=64, name="hidden")
-            nc.vector.tensor_scalar_max(out=hidden[c][:], in0=pre_acts[c][:], scalar1=0.0)
+        def relu_on_scalar(c):
+            edges = slice(0, SCALAR_RELU_SUBS * P)
+            nc.scalar.activation(out=grouped[c + 1][:, edges, :], in_=pre_acts[c][:, edges, :], func=ACT.Relu)
 
-        def quantise_h(c):
-            codes = work.tile([P, CHUNK], U32, align_bytes=64, name="h_codes")
-            scales = work.tile([P, CHUNK], U8, align_bytes=64, name="h_scales")
-            quantise(hidden[c], codes, scales)
-            h_codes[c], h_scales[c] = codes, scales
+        def relu_on_vector(c):
+            edges = slice(SCALAR_RELU_SUBS * P, CHUNK)
+            nc.vector.tensor_scalar_max(out=grouped[c + 1][:, edges, :], in0=pre_acts[c][:, edges, :], scalar1=0.0)
 
         def layer2(c):
             acc = layer2_psum.tile([P, CHUNK], F32, tag="layer2")
@@ -218,8 +225,8 @@ def tile_edgenetwork_kernel(
                 out=acc[:],
                 lhsT=w2_codes[:].bitcast(FP8X4),
                 lhsT_scale=w2_scales[:],
-                rhs=h_codes[c][:].bitcast(FP8X4),
-                rhs_scale=h_scales[c][:],
+                rhs=codes[c + 1][:, 0:CHUNK].bitcast(FP8X4),
+                rhs_scale=scales[c + 1][:, 0:CHUNK],
                 start=True,
                 stop=True,
             )
@@ -237,12 +244,9 @@ def tile_edgenetwork_kernel(
         def store(c):
             result = store_pool.tile([P, SUBS, OUT], F32)
             nc.scalar.copy(out=result[:], in_=out_back[c][:])
-            nc.scalar.dma_start(
+            nc.sync.dma_start(
                 out=out[c * CHUNK : (c + 1) * CHUNK, :].rearrange("(p s) o -> p s o", p=P), in_=result[:]
             )
-
-        def live(c):
-            return 0 <= c < N_CHUNKS
 
         for i in range(-3, N_CHUNKS + 2):
             ahead = i + 3
@@ -250,27 +254,30 @@ def tile_edgenetwork_kernel(
                 load_chunk(ahead + CHUNKS_AHEAD)
             if live(ahead + CHUNKS_PER_PIECE) and ahead % CHUNKS_PER_PIECE == 0:
                 load_edges(ahead // CHUNKS_PER_PIECE + 1)
+            if live(i) or live(i + 3):
+                grouped[i + 1] = work.tile([P, 2 * CHUNK, PACK], BF16, align_bytes=64, name="grouped")
             for half in range(2):
                 if live(i):
                     add_edge_term(i, 2 * half)
                     add_edge_term(i, 2 * half + 1)
+                    if half == 0:
+                        relu_on_scalar(i)
                 if live(i + 1):
                     layer1(i + 1, 2 * half)
                     layer1(i + 1, 2 * half + 1)
-                if half == 1 and live(i - 1):
-                    quantise_h(i - 1)
-                    layer2(i - 1)
                 if live(i + 3):
                     flip_x(i + 3, half)
                 if live(i - 2):
                     flip_back(i - 2, half)
             if live(i - 2):
                 store(i - 2)
-            if live(i + 2):
-                quantise_x(i + 2)
+            if live(i - 1) or live(i + 2):
+                quantise_step(i)
+            if live(i - 1):
+                layer2(i - 1)
             if live(i):
-                relu(i)
+                relu_on_vector(i)
             if i == -2:
                 prepare_layer2()
-            if live(i + 3):
+            if (i + 3) % TERM_CHUNKS == 0 and live(i + 3):
                 make_edge_term(i + 3)

@@ -19,13 +19,13 @@ M_TILES = MID // P
 CHUNK = 512
 SUBS = CHUNK // P
 N_CHUNKS = E // CHUNK
-CHUNKS_AHEAD = 4
-EDGE_PIECE = 2048
-CHUNKS_PER_PIECE = EDGE_PIECE // CHUNK
+BLOCK = 1024
+BLOCK_SUBS = BLOCK // P
+CHUNKS_PER_BLOCK = BLOCK // CHUNK
+N_BLOCKS = E // BLOCK
+BLOCKS_AHEAD = 2
 RUN = 4
 GPSIMD_M_TILES = 3
-TERM_CHUNKS = 2
-SCALAR_RELU_SUBS = 1
 
 FLOPS = 2 * E * ((D + 1) * MID + MID * OUT)
 
@@ -47,8 +47,8 @@ def tile_edgenetwork_kernel(
     with ExitStack() as stack:
         stack.enter_context(tc.manual_schedule())
         const = stack.enter_context(tc.tile_pool(name="const", bufs=1))
-        rows_pool = stack.enter_context(tc.tile_pool(name="rows", bufs=CHUNKS_AHEAD + 1))
-        term_pool = stack.enter_context(tc.tile_pool(name="term", bufs=2))
+        rows_pool = stack.enter_context(tc.tile_pool(name="rows", bufs=BLOCKS_AHEAD + 1))
+        term_pool = stack.enter_context(tc.tile_pool(name="term", bufs=3))
         work = stack.enter_context(tc.tile_pool(name="work", bufs=2))
         store_pool = stack.enter_context(tc.tile_pool(name="store", bufs=3))
         flip_psum = stack.enter_context(tc.psum_pool(name="flip_psum", bufs=2))
@@ -57,50 +57,50 @@ def tile_edgenetwork_kernel(
         back_psum = stack.enter_context(tc.psum_pool(name="back_psum", bufs=1))
 
         x_parts = (
-            (dst_node_feat, 0, F),
-            (dst_node_hidden, F, H),
-            (src_node_feat, F + H, F),
-            (src_node_hidden, 2 * F + H, H),
+            (dst_node_feat, 0, 0, F),
+            (dst_node_hidden, 0, F, P),
+            (dst_node_hidden, P, F + P, H - P),
+            (src_node_feat, 0, F + H, F),
+            (src_node_hidden, 0, 2 * F + H, P),
+            (src_node_hidden, P, 2 * F + H + P, H - P),
         )
         x_rows = {}
 
-        def load_chunk(c):
-            rows = rows_pool.tile([P, SUBS, D], BF16, name="x_rows")
-            for part, first, width in x_parts:
+        def load_block(b, subs):
+            if b not in x_rows:
+                x_rows[b] = rows_pool.tile([P, BLOCK_SUBS, D], BF16, name="x_rows")
+            for part, column, first, width in x_parts:
+                rows = part[b * BLOCK : (b + 1) * BLOCK, :].rearrange("(p s) k -> p s k", p=P)
                 nc.sync.dma_start(
-                    out=rows[:, :, first : first + width],
-                    in_=part[c * CHUNK : (c + 1) * CHUNK, :].rearrange("(p s) k -> p s k", p=P),
+                    out=x_rows[b][:, subs, first : first + width], in_=rows[:, subs, column : column + width]
                 )
-            x_rows[c] = rows
-
-        edge_all = const.tile([P, E], BF16)
-
-        def load_edges(q):
-            nc.sync.dma_start(
-                out=edge_all[:, q * EDGE_PIECE : (q + 1) * EDGE_PIECE],
-                in_=edge_feat[q * EDGE_PIECE : (q + 1) * EDGE_PIECE].partition_broadcast(P),
-            )
 
         w1_rows = const.tile([P, M_TILES, D + 2], BF16)
         nc.sync.dma_start(out=w1_rows[:, :, 0 : D + 1], in_=W1.rearrange("(p t) k -> p t k", t=M_TILES))
         b1_in = const.tile([P, M_TILES], BF16)
         nc.sync.dma_start(out=b1_in[:], in_=b1.rearrange("(p t) -> p t", t=M_TILES))
-        load_chunk(0)
-        load_edges(0)
+        edge_rows = const.tile([P, BLOCK], BF16)
+        nc.vector.memset(edge_rows[:], 0.0)
+        load_block(0, slice(0, SUBS))
+        nc.sync.dma_start(out=edge_rows[0:N_BLOCKS, :], in_=edge_feat.rearrange("(b j) -> b j", j=BLOCK))
+        load_block(0, slice(SUBS, BLOCK_SUBS))
         w2_rows = const.tile([P, MID], BF16)
         nc.sync.dma_start(out=w2_rows[:], in_=W2)
         b2_in = const.tile([P, 1], BF16)
         nc.sync.dma_start(out=b2_in[:], in_=b2.rearrange("(p o) -> p o", o=1))
-        for c in range(1, CHUNKS_AHEAD):
-            load_chunk(c)
+        for b in range(1, BLOCKS_AHEAD):
+            load_block(b, slice(0, SUBS))
+            load_block(b, slice(SUBS, BLOCK_SUBS))
 
         ident_f32 = const.tile([P, P], F32)
         make_identity(nc, ident_f32[:])
+        ident_bf16 = const.tile([P, P], BF16)
+        make_identity(nc, ident_bf16[:])
 
         def contraction_onto_partitions(row_words, grouped, first, half, copy):
             grouped_words = grouped[:].bitcast(F32)
             begin = first + 2 * half * P
-            flipped = flip_psum.tile([P, 2, 2, P], F32)
+            flipped = flip_psum.tile([P, 2, 2, P], F32, tag="flip", name="flipped")
             for s in range(2):
                 for u in range(2):
                     nc.tensor.transpose(
@@ -130,6 +130,9 @@ def tile_edgenetwork_kernel(
         w1_scales = const.tile([P, MID], U8, align_bytes=64)
         quantise(w1_grouped, w1_codes, w1_scales, slice(0, MID))
 
+        edge_columns = const.tile([P, BLOCK_SUBS, P], BF16)
+        nc.vector.tensor_copy(out=edge_columns[:], in_=edge_rows[:].rearrange("p (r s) -> p s r", s=BLOCK_SUBS))
+
         b2_col = const.tile([P, 1], F32)
         w2_grouped = const.tile([P, OUT, PACK], BF16, align_bytes=64)
         w2_codes = const.tile([P, OUT], U32, align_bytes=64)
@@ -145,35 +148,51 @@ def tile_edgenetwork_kernel(
             quantise(w2_grouped, w2_codes, w2_scales, slice(0, OUT))
 
         grouped, codes, scales = {}, {}, {}
-        edge_terms, layer1_banks, pre_acts, out_flipped, out_back = {}, {}, {}, {}, {}
+        edge_terms, layer1_banks, pre_acts, out_flipped, out_back, results = {}, {}, {}, {}, {}, {}
 
         def live(c):
             return 0 <= c < N_CHUNKS
 
+        def block_and_subs(c):
+            block, place = divmod(c, CHUNKS_PER_BLOCK)
+            return block, slice(place * SUBS, (place + 1) * SUBS)
+
         def flip_x(c, half):
-            x_words = x_rows[c][:].bitcast(F32)
+            block, subs = block_and_subs(c)
+            x_words = x_rows[block][:, subs, :].bitcast(F32)
             contraction_onto_partitions(lambda s: x_words[:, s, :], grouped[c - 2], CHUNK, half, nc.scalar.copy)
 
-        def make_edge_term(c):
-            term = term_pool.tile([P, M_TILES, TERM_CHUNKS, SUBS, P], F32, name="edge_term")
-            edges = edge_all[:, c * CHUNK : (c + TERM_CHUNKS) * CHUNK].rearrange(
-                "p (h r s) -> p h s r", h=TERM_CHUNKS, s=SUBS
+        def spread_edges(c):
+            block, subs = block_and_subs(c)
+            bank = flip_psum.tile([P, SUBS, P], BF16, tag="flip", name="edge_bank")
+            nc.tensor.matmul(
+                bank[:].rearrange("p s r -> p (s r)"),
+                lhsT=ident_bf16[:, block : block + 1].to_broadcast([P, P]),
+                rhs=edge_columns[:, subs, :].rearrange("p s r -> p (s r)"),
+                start=True,
+                stop=True,
             )
-            for h in range(TERM_CHUNKS):
-                edge_terms[c + h] = term[:, :, h, :, :]
+            edges = term_pool.tile([P, SUBS, P], BF16, name="edges")
+            nc.scalar.copy(out=edges[:], in_=bank[:])
+            return edges
+
+        def make_edge_term(c):
+            term = term_pool.tile([P, M_TILES, SUBS, P], F32, name="edge_term")
+            edge_terms[c] = term
+            edges = spread_edges(c)
             for t in range(M_TILES):
                 if t >= GPSIMD_M_TILES:
                     nc.scalar.activation(
-                        out=term[:, t, :, :, :],
-                        in_=edges,
+                        out=term[:, t, :, :],
+                        in_=edges[:],
                         func=ACT.Identity,
                         scale=w1_last[:, t : t + 1],
                         bias=b1_cols[:, t : t + 1],
                     )
                 else:
                     nc.gpsimd.tensor_scalar(
-                        out=term[:, t, :, :, :],
-                        in0=edges,
+                        out=term[:, t, :, :],
+                        in0=edges[:],
                         scalar1=w1_last[:, t : t + 1],
                         scalar2=b1_cols[:, t : t + 1],
                         op0=ALU.mult,
@@ -211,13 +230,8 @@ def tile_edgenetwork_kernel(
                 op=ALU.add,
             )
 
-        def relu_on_scalar(c):
-            edges = slice(0, SCALAR_RELU_SUBS * P)
-            nc.scalar.activation(out=grouped[c + 1][:, edges, :], in_=pre_acts[c][:, edges, :], func=ACT.Relu)
-
-        def relu_on_vector(c):
-            edges = slice(SCALAR_RELU_SUBS * P, CHUNK)
-            nc.vector.tensor_scalar_max(out=grouped[c + 1][:, edges, :], in0=pre_acts[c][:, edges, :], scalar1=0.0)
+        def relu(c):
+            nc.vector.tensor_scalar_max(out=grouped[c + 1][:, 0:CHUNK, :], in0=pre_acts[c][:], scalar1=0.0)
 
         def layer2(c):
             acc = layer2_psum.tile([P, CHUNK], F32, tag="layer2")
@@ -241,27 +255,27 @@ def tile_edgenetwork_kernel(
             for s in (2 * half, 2 * half + 1):
                 nc.tensor.transpose(out_back[c][:, s, :], out_flipped[c][:, s * P : (s + 1) * P], ident_f32[:])
 
-        def store(c):
-            result = store_pool.tile([P, SUBS, OUT], F32)
-            nc.scalar.copy(out=result[:], in_=out_back[c][:])
-            nc.sync.dma_start(
-                out=out[c * CHUNK : (c + 1) * CHUNK, :].rearrange("(p s) o -> p s o", p=P), in_=result[:]
-            )
+        def copy_result(c):
+            results[c] = store_pool.tile([P, SUBS, OUT], F32, name="result")
+            nc.scalar.copy(out=results[c][:], in_=out_back[c][:])
 
-        for i in range(-3, N_CHUNKS + 2):
+        def store(c):
+            block, subs = block_and_subs(c)
+            rows = out[block * BLOCK : (block + 1) * BLOCK, :].rearrange("(p s) o -> p s o", p=P)
+            nc.sync.dma_start(out=rows[:, subs, :], in_=results[c][:])
+
+        for i in range(-3, N_CHUNKS + 3):
             ahead = i + 3
-            if live(ahead + CHUNKS_AHEAD):
-                load_chunk(ahead + CHUNKS_AHEAD)
-            if live(ahead + CHUNKS_PER_PIECE) and ahead % CHUNKS_PER_PIECE == 0:
-                load_edges(ahead // CHUNKS_PER_PIECE + 1)
+            if live(i - 3):
+                store(i - 3)
+            if ahead % CHUNKS_PER_BLOCK == 0 and live(ahead + BLOCKS_AHEAD * CHUNKS_PER_BLOCK):
+                load_block(ahead // CHUNKS_PER_BLOCK + BLOCKS_AHEAD, slice(0, BLOCK_SUBS))
             if live(i) or live(i + 3):
                 grouped[i + 1] = work.tile([P, 2 * CHUNK, PACK], BF16, align_bytes=64, name="grouped")
             for half in range(2):
                 if live(i):
                     add_edge_term(i, 2 * half)
                     add_edge_term(i, 2 * half + 1)
-                    if half == 0:
-                        relu_on_scalar(i)
                 if live(i + 1):
                     layer1(i + 1, 2 * half)
                     layer1(i + 1, 2 * half + 1)
@@ -270,14 +284,14 @@ def tile_edgenetwork_kernel(
                 if live(i - 2):
                     flip_back(i - 2, half)
             if live(i - 2):
-                store(i - 2)
+                copy_result(i - 2)
             if live(i - 1) or live(i + 2):
                 quantise_step(i)
             if live(i - 1):
                 layer2(i - 1)
             if live(i):
-                relu_on_vector(i)
+                relu(i)
             if i == -2:
                 prepare_layer2()
-            if (i + 3) % TERM_CHUNKS == 0 and live(i + 3):
+            if live(i + 3):
                 make_edge_term(i + 3)

from contextlib import ExitStack

import concourse.mybir as mybir
from concourse.masks import make_identity

F32 = mybir.dt.float32
BF16 = mybir.dt.bfloat16
U32 = mybir.dt.uint32
U8 = mybir.dt.uint8
FP8X4 = mybir.dt.float8_e4m3fn_x4
ACT = mybir.ActivationFunctionType
ALU = mybir.AluOpType

P = 128
PACK = 4
E, F, H, MID, OUT = 16384, 64, 192, 512, 128
D = 2 * (F + H)
M_TILES = MID // P
CHUNK = 512
SUBS = CHUNK // P
N_CHUNKS = E // CHUNK
BLOCK = 1024
BLOCK_SUBS = BLOCK // P
CHUNKS_PER_BLOCK = BLOCK // CHUNK
N_BLOCKS = E // BLOCK
BLOCKS_AHEAD = 2
RUN = 4
GPSIMD_M_TILES = 3

FLOPS = 2 * E * ((D + 1) * MID + MID * OUT)


def tile_edgenetwork_kernel(
    tc,
    dst_node_feat,
    dst_node_hidden,
    src_node_feat,
    src_node_hidden,
    edge_feat,
    W1,
    b1,
    W2,
    b2,
    out,
):
    nc = tc.nc
    with ExitStack() as stack:
        stack.enter_context(tc.manual_schedule())
        const = stack.enter_context(tc.tile_pool(name="const", bufs=1))
        rows_pool = stack.enter_context(tc.tile_pool(name="rows", bufs=BLOCKS_AHEAD + 1))
        term_pool = stack.enter_context(tc.tile_pool(name="term", bufs=3))
        work = stack.enter_context(tc.tile_pool(name="work", bufs=2))
        store_pool = stack.enter_context(tc.tile_pool(name="store", bufs=3))
        flip_psum = stack.enter_context(tc.psum_pool(name="flip_psum", bufs=2))
        layer1_psum = stack.enter_context(tc.psum_pool(name="layer1_psum", bufs=M_TILES))
        layer2_psum = stack.enter_context(tc.psum_pool(name="layer2_psum", bufs=1))
        back_psum = stack.enter_context(tc.psum_pool(name="back_psum", bufs=1))

        x_parts = (
            (dst_node_feat, 0, 0, F),
            (dst_node_hidden, 0, F, P),
            (dst_node_hidden, P, F + P, H - P),
            (src_node_feat, 0, F + H, F),
            (src_node_hidden, 0, 2 * F + H, P),
            (src_node_hidden, P, 2 * F + H + P, H - P),
        )
        x_rows = {}

        def load_block(b, subs):
            if b not in x_rows:
                x_rows[b] = rows_pool.tile([P, BLOCK_SUBS, D], BF16, name="x_rows")
            for part, column, first, width in x_parts:
                rows = part[b * BLOCK : (b + 1) * BLOCK, :].rearrange("(p s) k -> p s k", p=P)
                nc.sync.dma_start(
                    out=x_rows[b][:, subs, first : first + width], in_=rows[:, subs, column : column + width]
                )

        w1_rows = const.tile([P, M_TILES, D + 2], BF16)
        nc.sync.dma_start(out=w1_rows[:, :, 0 : D + 1], in_=W1.rearrange("(p t) k -> p t k", t=M_TILES))
        b1_in = const.tile([P, M_TILES], BF16)
        nc.sync.dma_start(out=b1_in[:], in_=b1.rearrange("(p t) -> p t", t=M_TILES))
        edge_rows = const.tile([P, BLOCK], BF16)
        nc.vector.memset(edge_rows[:], 0.0)
        load_block(0, slice(0, SUBS))
        nc.sync.dma_start(out=edge_rows[0:N_BLOCKS, :], in_=edge_feat.rearrange("(b j) -> b j", j=BLOCK))
        load_block(0, slice(SUBS, BLOCK_SUBS))
        w2_rows = const.tile([P, MID], BF16)
        nc.sync.dma_start(out=w2_rows[:], in_=W2)
        b2_in = const.tile([P, 1], BF16)
        nc.sync.dma_start(out=b2_in[:], in_=b2.rearrange("(p o) -> p o", o=1))
        for b in range(1, BLOCKS_AHEAD):
            load_block(b, slice(0, SUBS))
            load_block(b, slice(SUBS, BLOCK_SUBS))

        ident_f32 = const.tile([P, P], F32)
        make_identity(nc, ident_f32[:])
        ident_bf16 = const.tile([P, P], BF16)
        make_identity(nc, ident_bf16[:])

        def contraction_onto_partitions(row_words, grouped, first, half, copy):
            grouped_words = grouped[:].bitcast(F32)
            begin = first + 2 * half * P
            flipped = flip_psum.tile([P, 2, 2, P], F32, tag="flip", name="flipped")
            for s in range(2):
                for u in range(2):
                    nc.tensor.transpose(
                        flipped[:, s, u, :], row_words(2 * half + s)[:, u : D // 2 : 2], ident_f32[:]
                    )
            copy(
                out=grouped_words[:, begin : begin + 2 * P, :].rearrange("p (s r) u -> p s r u", s=2),
                in_=flipped[:].rearrange("p s u r -> p s r u"),
            )

        def quantise(grouped, codes, scales, columns):
            nc.vector.quantize_mx(
                out=codes[:, columns].bitcast(FP8X4),
                scales=scales[:, columns],
                in_=grouped[:, columns, :].rearrange("p c j -> p (c j)"),
            )

        w1_last = const.tile([P, M_TILES], F32)
        nc.vector.tensor_copy(out=w1_last[:], in_=w1_rows[:, :, D])
        b1_cols = const.tile([P, M_TILES], F32)
        nc.vector.tensor_copy(out=b1_cols[:], in_=b1_in[:])
        w1_words = w1_rows[:].bitcast(F32)
        w1_grouped = const.tile([P, MID, PACK], BF16, align_bytes=64)
        for half in range(2):
            contraction_onto_partitions(lambda t: w1_words[:, t, 0 : D // 2], w1_grouped, 0, half, nc.vector.tensor_copy)
        w1_codes = const.tile([P, MID], U32, align_bytes=64)
        w1_scales = const.tile([P, MID], U8, align_bytes=64)
        quantise(w1_grouped, w1_codes, w1_scales, slice(0, MID))

        edge_columns = const.tile([P, BLOCK_SUBS, P], BF16)
        nc.vector.tensor_copy(out=edge_columns[:], in_=edge_rows[:].rearrange("p (r s) -> p s r", s=BLOCK_SUBS))

        b2_col = const.tile([P, 1], F32)
        w2_grouped = const.tile([P, OUT, PACK], BF16, align_bytes=64)
        w2_codes = const.tile([P, OUT], U32, align_bytes=64)
        w2_scales = const.tile([P, OUT], U8, align_bytes=64)

        def prepare_layer2():
            w2_words = w2_rows[:].bitcast(F32)
            w2_flipped = back_psum.tile([P, 2, OUT], F32, tag="back", name="w2_flipped")
            for u in range(2):
                nc.tensor.transpose(w2_flipped[:, u, :], w2_words[:, u : MID // 2 : 2], ident_f32[:])
            nc.vector.tensor_copy(out=w2_grouped[:].bitcast(F32), in_=w2_flipped[:].rearrange("p u o -> p o u"))
            nc.vector.tensor_copy(out=b2_col[:], in_=b2_in[:])
            quantise(w2_grouped, w2_codes, w2_scales, slice(0, OUT))

        grouped, codes, scales = {}, {}, {}
        edge_terms, layer1_banks, pre_acts, out_flipped, out_back, results = {}, {}, {}, {}, {}, {}

        def live(c):
            return 0 <= c < N_CHUNKS

        def block_and_subs(c):
            block, place = divmod(c, CHUNKS_PER_BLOCK)
            return block, slice(place * SUBS, (place + 1) * SUBS)

        def flip_x(c, half):
            block, subs = block_and_subs(c)
            x_words = x_rows[block][:, subs, :].bitcast(F32)
            contraction_onto_partitions(lambda s: x_words[:, s, :], grouped[c - 2], CHUNK, half, nc.scalar.copy)

        def spread_edges(c):
            block, subs = block_and_subs(c)
            bank = flip_psum.tile([P, SUBS, P], BF16, tag="flip", name="edge_bank")
            nc.tensor.matmul(
                bank[:].rearrange("p s r -> p (s r)"),
                lhsT=ident_bf16[:, block : block + 1].to_broadcast([P, P]),
                rhs=edge_columns[:, subs, :].rearrange("p s r -> p (s r)"),
                start=True,
                stop=True,
            )
            edges = term_pool.tile([P, SUBS, P], BF16, name="edges")
            nc.scalar.copy(out=edges[:], in_=bank[:])
            return edges

        def make_edge_term(c):
            term = term_pool.tile([P, M_TILES, SUBS, P], F32, name="edge_term")
            edge_terms[c] = term
            edges = spread_edges(c)
            for t in range(M_TILES):
                if t >= GPSIMD_M_TILES:
                    nc.scalar.activation(
                        out=term[:, t, :, :],
                        in_=edges[:],
                        func=ACT.Identity,
                        scale=w1_last[:, t : t + 1],
                        bias=b1_cols[:, t : t + 1],
                    )
                else:
                    nc.gpsimd.tensor_scalar(
                        out=term[:, t, :, :],
                        in0=edges[:],
                        scalar1=w1_last[:, t : t + 1],
                        scalar2=b1_cols[:, t : t + 1],
                        op0=ALU.mult,
                        op1=ALU.add,
                    )

        def quantise_step(i):
            codes[i] = work.tile([P, 2 * CHUNK], U32, align_bytes=64, name="codes")
            scales[i] = work.tile([P, 2 * CHUNK], U8, align_bytes=64, name="scales")
            columns = slice(0 if live(i - 1) else CHUNK, 2 * CHUNK if live(i + 2) else CHUNK)
            quantise(grouped[i], codes[i], scales[i], columns)

        def layer1(c, s):
            bank = layer1_psum.tile([P, M_TILES, P], F32, name="layer1_bank")
            edges = slice(CHUNK + s * P, CHUNK + (s + 1) * P)
            for t in range(M_TILES):
                nc.tensor.matmul_mx(
                    out=bank[:, t, :],
                    lhsT=w1_codes[:, t * P : (t + 1) * P].bitcast(FP8X4),
                    lhsT_scale=w1_scales[:, t * P : (t + 1) * P],
                    rhs=codes[c - 2][:, edges].bitcast(FP8X4),
                    rhs_scale=scales[c - 2][:, edges],
                    start=True,
                    stop=True,
                )
            layer1_banks[c, s] = bank

        def add_edge_term(c, s):
            if s == 0:
                pre_acts[c] = work.tile([P, CHUNK, PACK], BF16, align_bytes=64, name="pre_act")
            nc.vector.tensor_tensor(
                out=pre_acts[c][:, s * P : (s + 1) * P, :].rearrange("p (g i) t -> p g t i", i=RUN),
                in0=layer1_banks[c, s][:].rearrange("p t (g i) -> p g t i", i=RUN),
                in1=edge_terms[c][:, :, s, :].rearrange("p t (g i) -> p g t i", i=RUN),
                op=ALU.add,
            )

        def relu(c):
            nc.vector.tensor_scalar_max(out=grouped[c + 1][:, 0:CHUNK, :], in0=pre_acts[c][:], scalar1=0.0)

        def layer2(c):
            acc = layer2_psum.tile([P, CHUNK], F32, tag="layer2")
            nc.tensor.matmul_mx(
                out=acc[:],
                lhsT=w2_codes[:].bitcast(FP8X4),
                lhsT_scale=w2_scales[:],
                rhs=codes[c + 1][:, 0:CHUNK].bitcast(FP8X4),
                rhs_scale=scales[c + 1][:, 0:CHUNK],
                start=True,
                stop=True,
            )
            out_flipped[c] = work.tile([P, CHUNK], F32, name="out_flipped")
            nc.scalar.activation(
                out=out_flipped[c][:], in_=acc[:], func=ACT.Tanh, bias=b2_col[:], scale=1.0
            )

        def flip_back(c, half):
            if half == 0:
                out_back[c] = back_psum.tile([P, SUBS, OUT], F32, tag="back", name="out_back")
            for s in (2 * half, 2 * half + 1):
                nc.tensor.transpose(out_back[c][:, s, :], out_flipped[c][:, s * P : (s + 1) * P], ident_f32[:])

        def copy_result(c):
            results[c] = store_pool.tile([P, SUBS, OUT], F32, name="result")
            nc.scalar.copy(out=results[c][:], in_=out_back[c][:])

        def store(c):
            block, subs = block_and_subs(c)
            rows = out[block * BLOCK : (block + 1) * BLOCK, :].rearrange("(p s) o -> p s o", p=P)
            nc.sync.dma_start(out=rows[:, subs, :], in_=results[c][:])

        for i in range(-3, N_CHUNKS + 3):
            ahead = i + 3
            if live(i - 3):
                store(i - 3)
            if ahead % CHUNKS_PER_BLOCK == 0 and live(ahead + BLOCKS_AHEAD * CHUNKS_PER_BLOCK):
                load_block(ahead // CHUNKS_PER_BLOCK + BLOCKS_AHEAD, slice(0, BLOCK_SUBS))
            if live(i) or live(i + 3):
                grouped[i + 1] = work.tile([P, 2 * CHUNK, PACK], BF16, align_bytes=64, name="grouped")
            for half in range(2):
                if live(i):
                    add_edge_term(i, 2 * half)
                    add_edge_term(i, 2 * half + 1)
                if live(i + 1):
                    layer1(i + 1, 2 * half)
                    layer1(i + 1, 2 * half + 1)
                if live(i + 3):
                    flip_x(i + 3, half)
                if live(i - 2):
                    flip_back(i - 2, half)
            if live(i - 2):
                copy_result(i - 2)
            if live(i - 1) or live(i + 2):
                quantise_step(i)
            if live(i - 1):
                layer2(i - 1)
            if live(i):
                relu(i)
            if i == -2:
                prepare_layer2()
            if live(i + 3):
                make_edge_term(i + 3)
